import numpy as np
import ml_dtypes


def mxq(x, axis, fmt="e4m3"):
    dtype, down = {"e4m3": (ml_dtypes.float8_e4m3fn, 7), "e5m2": (ml_dtypes.float8_e5m2, 14)}[fmt]
    v = np.moveaxis(np.asarray(x, np.float32).astype(ml_dtypes.bfloat16).astype(np.float64), axis, -1)
    blocks = v.reshape(v.shape[:-1] + (-1, 32))
    amax = np.abs(blocks).max(-1, keepdims=True)
    byte = np.maximum(np.where(amax > 0, np.frexp(amax)[1] - 1 + 127, 0) - down, 1)
    scale = np.exp2(byte - 127.0)
    codes = (blocks / scale).astype(np.float32).astype(dtype).astype(np.float64)
    return np.moveaxis((codes * scale).reshape(v.shape), -1, axis)


WIDE = False


def mx_kscale(k):
    if not WIDE:
        return np.ones(k)
    levels = np.array([10, -10, 5, -5, 0])
    a = np.random.permutation(np.resize(levels, k // 512 * 4)).reshape(k // 512, 4)
    idx = np.arange(k)
    return np.exp2(a[idx // 512, idx % 128 // 32])


BF16 = ml_dtypes.bfloat16


def bf(x):
    return np.asarray(x, np.float32).astype(BF16)


def f64(x):
    return np.asarray(x).astype(np.float64)


B, H, W, C, NH, WS, SHIFT, MR = 1, 64, 64, 256, 8, 32, 16, 4
HD = C // NH
WS2 = WS * WS
NWH, NWW = H // WS, W // WS
EPS = 1e-5
G2 = 0.1


def layer_norm(v, w, b):
    mu = v.mean(-1, keepdims=True)
    var = ((v - mu) ** 2).mean(-1, keepdims=True)
    return (v - mu) * (1.0 / np.sqrt(var + EPS)) * w + b


def setup_inputs():
    s = mx_kscale(WS2)
    u = (s / s.max()) ** 2
    um = np.tile(u.reshape(WS, WS), (NWH, NWW)).reshape(1, H * W, 1)
    d = u * np.sqrt((G2 + EPS) / (G2 * u * u + EPS))
    g = np.exp2(-7.5 * np.random.random_sample((B, H * W, 1)))
    x = (np.random.standard_normal((B, H * W, C)) + 0.5 * np.random.standard_normal((B, H * W, 1))) * g * um
    return {"x": bf(x),
            "norm1_w": bf(1.0 + 0.2 * np.random.standard_normal(C)),
            "norm1_b": bf(0.2 * np.random.standard_normal(C) * d.min()),
            "spatial_w": bf(np.random.standard_normal((NH, WS2, WS2)) / np.sqrt(WS2) / d[None, None, :]),
            "spatial_b": bf(0.3 * np.random.standard_normal((NH, WS2)))}


def reference(x, norm1_w, norm1_b, spatial_w, spatial_b):
    x = f64(x)
    xn = layer_norm(x, f64(norm1_w), f64(norm1_b))
    win = xn.reshape(B, NWH, WS, NWW, WS, C).transpose(0, 1, 3, 2, 4, 5).reshape(-1, WS2, NH, HD)
    wh = win.transpose(0, 2, 1, 3)
    out = (mxq(f64(spatial_w), 2, "e4m3")[None] @ mxq(wh, 2, "e4m3")) + f64(spatial_b)[None, :, :, None]
    w2 = out.transpose(0, 2, 1, 3).reshape(B, NWH, NWW, WS, WS, C)
    xs2 = w2.transpose(0, 1, 3, 2, 4, 5).reshape(B, H * W, C)
    return x + xs2

@@ -1,0 +1,198 @@
+from contextlib import ExitStack
+
+import concourse.mybir as mybir
+from concourse.masks import make_identity
+
+F32 = mybir.dt.float32
+BF16 = mybir.dt.bfloat16
+U32 = mybir.dt.uint32
+U8 = mybir.dt.uint8
+FP8X4 = mybir.dt.float8_e4m3fn_x4
+ALU = mybir.AluOpType
+ACT = mybir.ActivationFunctionType
+
+P = 128
+C = 256
+HEADS = 8
+HEAD_DIM = C // HEADS
+WINDOWS = 4
+TOKENS = 1024
+PAIR = 2
+SLICES = TOKENS // (PAIR * P)
+PASSES = 2
+PACK = 4
+HEADS_PER_LOAD = 4
+EPS = 1e-5
+
+FLOPS = 2 * HEADS * WINDOWS * TOKENS * TOKENS * HEAD_DIM
+
+
+def window_view(tokens_by_channels):
+    return tokens_by_channels.rearrange(
+        "b (wr a qh wc ql e) c -> (b wr) wc a qh ql (e c)", wr=2, a=SLICES, qh=8, wc=2, ql=16, e=PAIR
+    )
+
+
+def tile_swinmlpblocknew_pa_kernel(tc, x, norm1_w, norm1_b, spatial_w, spatial_b, out):
+    nc = tc.nc
+    x_windows = window_view(x)
+    out_windows = window_view(out)
+
+    with ExitStack() as ctx:
+        keep = ctx.enter_context(tc.tile_pool(name="keep", bufs=1))
+        norm_pool = ctx.enter_context(tc.tile_pool(name="norm", bufs=2))
+        weight_pool = ctx.enter_context(tc.tile_pool(name="weights", bufs=5))
+        grouped_pool = ctx.enter_context(tc.tile_pool(name="grouped", bufs=4))
+        codes_pool = ctx.enter_context(tc.tile_pool(name="codes", bufs=4))
+        out_pool = ctx.enter_context(tc.tile_pool(name="outs", bufs=2))
+        psum_words = ctx.enter_context(tc.psum_pool(name="psum_words", bufs=6))
+        psum_acc = ctx.enter_context(tc.psum_pool(name="psum_acc", bufs=2))
+
+        x_sb = keep.tile([P, WINDOWS, SLICES, PAIR * C], BF16)
+        for n in range(WINDOWS):
+            for a in range(SLICES):
+                nc.sync.dma_start(out=x_sb[:, n, a, :], in_=x_windows[n // 2, n % 2, a])
+
+        ident = keep.tile([P, P], F32)
+        make_identity(nc, ident[:])
+        gain_bc = keep.tile([P, C], BF16)
+        nc.scalar.dma_start(out=gain_bc[:], in_=norm1_w.partition_broadcast(P))
+        shift_bc = keep.tile([P, C], BF16)
+        nc.scalar.dma_start(out=shift_bc[:], in_=norm1_b.partition_broadcast(P))
+
+        bias_rows = keep.tile([P, PAIR * P], BF16)
+        nc.vector.memset(bias_rows[:], 0.0)
+        nc.scalar.dma_start(
+            out=bias_rows[0 : HEADS * SLICES, :], in_=spatial_b.rearrange("h (a w) -> (h a) w", a=SLICES)
+        )
+        bias_ps = psum_words.tile([P, PACK, P], F32, tag="words")
+        nc.tensor.transpose(out=bias_ps[:, 0, :], in_=bias_rows[:].bitcast(F32), identity=ident[:])
+        bias_col = keep.tile([P, HEADS, SLICES, PAIR], F32)
+        nc.vector.tensor_copy(
+            out=bias_col[:].rearrange("p h a e -> p (h a e)"),
+            in_=bias_ps[:, 0, 0 : HEADS * SLICES].bitcast(BF16),
+        )
+
+        xn_grouped = keep.tile([P, PASSES, HEADS, WINDOWS, HEAD_DIM * PACK], BF16, align_bytes=64)
+        stats = keep.tile([P, WINDOWS, SLICES, 3 * PAIR], F32)
+        var_eps = keep.tile([P, WINDOWS, SLICES, PAIR], F32)
+        std = keep.tile([P, WINDOWS, SLICES, PAIR], F32)
+        rstd = keep.tile([P, WINDOWS, SLICES, PAIR], F32)
+        minus_mean_rstd = keep.tile([P, WINDOWS, SLICES, PAIR], F32)
+        for n in range(WINDOWS):
+            for a in range(SLICES):
+                nc.vector.bn_stats(
+                    out=stats[:, n, a, :], in_=x_sb[:, n, a, :].rearrange("q (e c) -> q c e", e=PAIR)
+                )
+            moments = stats[:, n, :, :].rearrange("q a (e k) -> q a e k", k=3)
+            nc.vector.tensor_scalar(
+                out=var_eps[:, n],
+                in0=moments[:, :, :, 2],
+                scalar1=1.0 / C,
+                scalar2=EPS,
+                op0=ALU.mult,
+                op1=ALU.add,
+            )
+            nc.scalar.sqrt(out=std[:, n], in_=var_eps[:, n])
+            nc.vector.reciprocal(out=rstd[:, n], in_=std[:, n])
+            nc.vector.scalar_tensor_tensor(
+                out=minus_mean_rstd[:, n],
+                in0=moments[:, :, :, 1],
+                scalar=-1.0,
+                in1=rstd[:, n],
+                op0=ALU.mult,
+                op1=ALU.mult,
+            )
+            normed = norm_pool.tile([P, SLICES * PAIR, C], F32)
+            for a in range(SLICES):
+                for e in range(PAIR):
+                    nc.scalar.activation(
+                        out=normed[:, PAIR * a + e, :],
+                        in_=x_sb[:, n, a, e * C : (e + 1) * C],
+                        func=ACT.Identity,
+                        scale=rstd[:, n, a, e : e + 1],
+                        bias=minus_mean_rstd[:, n, a, e : e + 1],
+                    )
+            nc.vector.tensor_tensor(
+                out=normed[:],
+                in0=normed[:],
+                in1=gain_bc[:].unsqueeze(1).to_broadcast([P, SLICES * PAIR, C]),
+                op=ALU.mult,
+            )
+            for g in range(PASSES):
+                nc.vector.tensor_tensor(
+                    out=xn_grouped[:, g, :, n, :].rearrange("q h (d j) -> q h d j", j=PACK),
+                    in0=normed[:, PACK * g : PACK * (g + 1), :].rearrange("q j (h d) -> q h d j", h=HEADS),
+                    in1=shift_bc[:]
+                    .rearrange("q (h d) -> q h d", h=HEADS)
+                    .unsqueeze(3)
+                    .to_broadcast([P, HEADS, HEAD_DIM, PACK]),
+                    op=ALU.add,
+                )
+
+        x_codes = keep.tile([P, PASSES, HEADS * P], U32, align_bytes=64)
+        x_scales = keep.tile([P, PASSES, HEADS * P], U8, align_bytes=64)
+        for g in range(PASSES):
+            nc.vector.quantize_mx(
+                out=x_codes[:, g, :].bitcast(FP8X4),
+                scales=x_scales[:, g, :],
+                in_=xn_grouped[:, g].rearrange("q h n f -> q (h n f)"),
+            )
+
+        for a in range(SLICES):
+            out_sb = out_pool.tile([P, WINDOWS, PAIR, C], F32)
+            for first_head in range(0, HEADS, HEADS_PER_LOAD):
+                w_raw = weight_pool.tile([P, HEADS_PER_LOAD, PAIR, TOKENS], BF16)
+                nc.sync.dma_start(
+                    out=w_raw[:].rearrange("p i e t -> p i (e t)"),
+                    in_=spatial_w[
+                        first_head : first_head + HEADS_PER_LOAD, PAIR * P * a : PAIR * P * (a + 1), :
+                    ].rearrange("i (p e) t -> p i (e t)", e=PAIR),
+                )
+                for e in range(PAIR):
+                    w_grouped = grouped_pool.tile([P, HEADS_PER_LOAD, PASSES * P * PACK], BF16, align_bytes=64)
+                    for i in range(HEADS_PER_LOAD):
+                        row_words = w_raw[:, i, e, :].bitcast(F32)
+                        words_ps = psum_words.tile([P, PACK, P], F32, tag="words")
+                        for k in range(SLICES):
+                            nc.tensor.transpose(
+                                out=words_ps[:, k, :], in_=row_words[:, k * P : (k + 1) * P], identity=ident[:]
+                            )
+                        nc.scalar.copy(
+                            out=w_grouped[:, i, :].bitcast(F32).rearrange("q (g s u) -> q g s u", g=PASSES, u=2),
+                            in_=words_ps[:].rearrange("q (g u) s -> q g s u", g=PASSES),
+                        )
+                    w_codes = codes_pool.tile([P, HEADS_PER_LOAD, PASSES, P], U32, align_bytes=64)
+                    w_scales = codes_pool.tile([P, HEADS_PER_LOAD, PASSES, P], U8, align_bytes=64)
+                    nc.vector.quantize_mx(
+                        out=w_codes[:].rearrange("q i g s -> q (i g s)").bitcast(FP8X4),
+                        scales=w_scales[:].rearrange("q i g s -> q (i g s)"),
+                        in_=w_grouped[:].rearrange("q i f -> q (i f)"),
+                    )
+                    acc = psum_acc.tile([P, HEADS_PER_LOAD, P], F32)
+                    for i in range(HEADS_PER_LOAD):
+                        h = first_head + i
+                        for g in range(PASSES):
+                            nc.tensor.matmul_mx(
+                                out=acc[:, i, :],
+                                lhsT=w_codes[:, i, g, :].bitcast(FP8X4),
+                                lhsT_scale=w_scales[:, i, g, :],
+                                rhs=x_codes[:, g, h * P : (h + 1) * P].bitcast(FP8X4),
+                                rhs_scale=x_scales[:, g, h * P : (h + 1) * P],
+                                start=(g == 0),
+                                stop=(g == PASSES - 1),
+                            )
+                    for i in range(HEADS_PER_LOAD):
+                        h = first_head + i
+                        nc.vector.scalar_tensor_tensor(
+                            out=out_sb[:, :, e, h * HEAD_DIM : (h + 1) * HEAD_DIM],
+                            in0=acc[:, i, :].rearrange("p (n d) -> p n d", n=WINDOWS),
+                            scalar=bias_col[:, h, a, e : e + 1],
+                            in1=x_sb[:, :, a, e * C + h * HEAD_DIM : e * C + (h + 1) * HEAD_DIM],
+                            op0=ALU.add,
+                            op1=ALU.add,
+                        )
+            for n in range(WINDOWS):
+                nc.sync.dma_start(
+                    out=out_windows[n // 2, n % 2, a], in_=out_sb[:, n].rearrange("p e c -> p (e c)")
+                )

@@ -55,10 +55,18 @@ def tile_swinmlpblocknew_pa_kernel(tc, x, norm1_w, norm1_b, spatial_w, spatial_b
 
         ident = keep.tile([P, P], F32)
         make_identity(nc, ident[:])
-        gain_bc = keep.tile([P, C], BF16)
-        nc.scalar.dma_start(out=gain_bc[:], in_=norm1_w.partition_broadcast(P))
-        shift_bc = keep.tile([P, C], BF16)
-        nc.scalar.dma_start(out=shift_bc[:], in_=norm1_b.partition_broadcast(P))
+        norm_rows = keep.tile([P, 2 * C], BF16)
+        nc.vector.memset(norm_rows[:], 0.0)
+        nc.scalar.dma_start(out=norm_rows[0:1, 0:C], in_=norm1_w.unsqueeze(0))
+        nc.scalar.dma_start(out=norm_rows[0:1, C : 2 * C], in_=norm1_b.unsqueeze(0))
+        ones = keep.tile([P, P], BF16)
+        nc.vector.memset(ones[:], 1.0)
+        norm_ps = psum_words.tile([P, 2 * C], F32, tag="words")
+        nc.tensor.matmul(out=norm_ps[:], lhsT=ones[:], rhs=norm_rows[:], start=True, stop=True)
+        norm_bc = keep.tile([P, 2 * C], F32)
+        nc.scalar.copy(out=norm_bc[:], in_=norm_ps[:])
+        gain_bc = norm_bc[:, 0:C]
+        shift_bc = norm_bc[:, C : 2 * C]
 
         bias_rows = keep.tile([P, PAIR * P], BF16)
         nc.vector.memset(bias_rows[:], 0.0)
@@ -116,14 +124,14 @@ def tile_swinmlpblocknew_pa_kernel(tc, x, norm1_w, norm1_b, spatial_w, spatial_b
             nc.vector.tensor_tensor(
                 out=normed[:],
                 in0=normed[:],
-                in1=gain_bc[:].unsqueeze(1).to_broadcast([P, SLICES * PAIR, C]),
+                in1=gain_bc.unsqueeze(1).to_broadcast([P, SLICES * PAIR, C]),
                 op=ALU.mult,
             )
             for g in range(PASSES):
                 nc.vector.tensor_tensor(
                     out=xn_grouped[:, g, :, n, :].rearrange("q h (d j) -> q h d j", j=PACK),
                     in0=normed[:, PACK * g : PACK * (g + 1), :].rearrange("q j (h d) -> q h d j", h=HEADS),
-                    in1=shift_bc[:]
+                    in1=shift_bc
                     .rearrange("q (h d) -> q h d", h=HEADS)
                     .unsqueeze(3)
                     .to_broadcast([P, HEADS, HEAD_DIM, PACK]),

@@ -22,6 +22,10 @@ SLICES = TOKENS // (PAIR * P)
 PASSES = 2
 PACK = 4
 HEADS_PER_LOAD = 4
+LOADS = SLICES * HEADS // HEADS_PER_LOAD
+GROUPS = LOADS * PAIR
+AHEAD = 4
+WEIGHT_BUFS = 5
 EPS = 1e-5
 
 FLOPS = 2 * HEADS * WINDOWS * TOKENS * TOKENS * HEAD_DIM
@@ -41,53 +45,40 @@ def tile_swinmlpblocknew_pa_kernel(tc, x, norm1_w, norm1_b, spatial_w, spatial_b
     with ExitStack() as ctx:
         keep = ctx.enter_context(tc.tile_pool(name="keep", bufs=1))
         norm_pool = ctx.enter_context(tc.tile_pool(name="norm", bufs=2))
-        weight_pool = ctx.enter_context(tc.tile_pool(name="weights", bufs=5))
-        grouped_pool = ctx.enter_context(tc.tile_pool(name="grouped", bufs=4))
-        codes_pool = ctx.enter_context(tc.tile_pool(name="codes", bufs=4))
+        weight_pool = ctx.enter_context(tc.tile_pool(name="weights", bufs=WEIGHT_BUFS))
+        grouped_pool = ctx.enter_context(tc.tile_pool(name="grouped", bufs=AHEAD))
+        codes_pool = ctx.enter_context(tc.tile_pool(name="codes", bufs=3))
         out_pool = ctx.enter_context(tc.tile_pool(name="outs", bufs=2))
         psum_words = ctx.enter_context(tc.psum_pool(name="psum_words", bufs=6))
         psum_acc = ctx.enter_context(tc.psum_pool(name="psum_acc", bufs=2))
+        ctx.enter_context(tc.manual_schedule())
 
         x_sb = keep.tile([P, WINDOWS, SLICES, PAIR * C], BF16)
-        for n in range(WINDOWS):
-            for a in range(SLICES):
-                nc.sync.dma_start(out=x_sb[:, n, a, :], in_=x_windows[n // 2, n % 2, a])
-
         ident = keep.tile([P, P], F32)
-        make_identity(nc, ident[:])
-        norm_rows = keep.tile([P, 2 * C], BF16)
-        nc.vector.memset(norm_rows[:], 0.0)
-        nc.scalar.dma_start(out=norm_rows[0:1, 0:C], in_=norm1_w.unsqueeze(0))
-        nc.scalar.dma_start(out=norm_rows[0:1, C : 2 * C], in_=norm1_b.unsqueeze(0))
         ones = keep.tile([P, P], BF16)
-        nc.vector.memset(ones[:], 1.0)
-        norm_ps = psum_words.tile([P, 2 * C], F32, tag="words")
-        nc.tensor.matmul(out=norm_ps[:], lhsT=ones[:], rhs=norm_rows[:], start=True, stop=True)
+        norm_rows = keep.tile([P, 2 * C], BF16)
         norm_bc = keep.tile([P, 2 * C], F32)
-        nc.scalar.copy(out=norm_bc[:], in_=norm_ps[:])
-        gain_bc = norm_bc[:, 0:C]
-        shift_bc = norm_bc[:, C : 2 * C]
-
         bias_rows = keep.tile([P, PAIR * P], BF16)
-        nc.vector.memset(bias_rows[:], 0.0)
-        nc.scalar.dma_start(
-            out=bias_rows[0 : HEADS * SLICES, :], in_=spatial_b.rearrange("h (a w) -> (h a) w", a=SLICES)
-        )
-        bias_ps = psum_words.tile([P, PACK, P], F32, tag="words")
-        nc.tensor.transpose(out=bias_ps[:, 0, :], in_=bias_rows[:].bitcast(F32), identity=ident[:])
         bias_col = keep.tile([P, HEADS, SLICES, PAIR], F32)
-        nc.vector.tensor_copy(
-            out=bias_col[:].rearrange("p h a e -> p (h a e)"),
-            in_=bias_ps[:, 0, 0 : HEADS * SLICES].bitcast(BF16),
-        )
-
-        xn_grouped = keep.tile([P, PASSES, HEADS, WINDOWS, HEAD_DIM * PACK], BF16, align_bytes=64)
         stats = keep.tile([P, WINDOWS, SLICES, 3 * PAIR], F32)
         var_eps = keep.tile([P, WINDOWS, SLICES, PAIR], F32)
         std = keep.tile([P, WINDOWS, SLICES, PAIR], F32)
         rstd = keep.tile([P, WINDOWS, SLICES, PAIR], F32)
         minus_mean_rstd = keep.tile([P, WINDOWS, SLICES, PAIR], F32)
-        for n in range(WINDOWS):
+        xn_grouped = keep.tile([P, PASSES, HEADS, WINDOWS, HEAD_DIM * PACK], BF16, align_bytes=64)
+        x_codes = keep.tile([P, PASSES, HEADS * P], U32, align_bytes=64)
+        x_scales = keep.tile([P, PASSES, HEADS * P], U8, align_bytes=64)
+
+        normed = {}
+        w_raw = {}
+        words_ps = {}
+        w_grouped = {}
+        w_codes = {}
+        w_scales = {}
+        acc = {}
+        out_sb = {}
+
+        def statistics(n):
             for a in range(SLICES):
                 nc.vector.bn_stats(
                     out=stats[:, n, a, :], in_=x_sb[:, n, a, :].rearrange("q (e c) -> q c e", e=PAIR)
@@ -102,6 +93,9 @@ def tile_swinmlpblocknew_pa_kernel(tc, x, norm1_w, norm1_b, spatial_w, spatial_b
                 op1=ALU.add,
             )
             nc.scalar.sqrt(out=std[:, n], in_=var_eps[:, n])
+
+        def scales(n):
+            moments = stats[:, n, :, :].rearrange("q a (e k) -> q a e k", k=3)
             nc.vector.reciprocal(out=rstd[:, n], in_=std[:, n])
             nc.vector.scalar_tensor_tensor(
                 out=minus_mean_rstd[:, n],
@@ -111,35 +105,169 @@ def tile_swinmlpblocknew_pa_kernel(tc, x, norm1_w, norm1_b, spatial_w, spatial_b
                 op0=ALU.mult,
                 op1=ALU.mult,
             )
-            normed = norm_pool.tile([P, SLICES * PAIR, C], F32)
+
+        def normalise(n):
+            normed_n = norm_pool.tile([P, SLICES * PAIR, C], F32, tag="normed")
+            normed[n] = normed_n
             for a in range(SLICES):
                 for e in range(PAIR):
                     nc.scalar.activation(
-                        out=normed[:, PAIR * a + e, :],
+                        out=normed_n[:, PAIR * a + e, :],
                         in_=x_sb[:, n, a, e * C : (e + 1) * C],
                         func=ACT.Identity,
                         scale=rstd[:, n, a, e : e + 1],
                         bias=minus_mean_rstd[:, n, a, e : e + 1],
                     )
+
+        def gain_and_shift(n):
             nc.vector.tensor_tensor(
-                out=normed[:],
-                in0=normed[:],
-                in1=gain_bc.unsqueeze(1).to_broadcast([P, SLICES * PAIR, C]),
+                out=normed[n][:],
+                in0=normed[n][:],
+                in1=norm_bc[:, 0:C].unsqueeze(1).to_broadcast([P, SLICES * PAIR, C]),
                 op=ALU.mult,
             )
             for g in range(PASSES):
                 nc.vector.tensor_tensor(
                     out=xn_grouped[:, g, :, n, :].rearrange("q h (d j) -> q h d j", j=PACK),
-                    in0=normed[:, PACK * g : PACK * (g + 1), :].rearrange("q j (h d) -> q h d j", h=HEADS),
-                    in1=shift_bc
+                    in0=normed[n][:, PACK * g : PACK * (g + 1), :].rearrange("q j (h d) -> q h d j", h=HEADS),
+                    in1=norm_bc[:, C : 2 * C]
                     .rearrange("q (h d) -> q h d", h=HEADS)
                     .unsqueeze(3)
                     .to_broadcast([P, HEADS, HEAD_DIM, PACK]),
                     op=ALU.add,
                 )
 
-        x_codes = keep.tile([P, PASSES, HEADS * P], U32, align_bytes=64)
-        x_scales = keep.tile([P, PASSES, HEADS * P], U8, align_bytes=64)
+        def load_weights(c):
+            a = c // 2
+            first_head = HEADS_PER_LOAD * (c % 2)
+            w_raw_c = weight_pool.tile([P, HEADS_PER_LOAD, PAIR, TOKENS], BF16, tag="w_raw")
+            w_raw[c] = w_raw_c
+            nc.sync.dma_start(
+                out=w_raw_c[:].rearrange("p i e t -> p i (e t)"),
+                in_=spatial_w[
+                    first_head : first_head + HEADS_PER_LOAD, PAIR * P * a : PAIR * P * (a + 1), :
+                ].rearrange("i (p e) t -> p i (e t)", e=PAIR),
+            )
+
+        def transpose_group(k):
+            for i in range(HEADS_PER_LOAD):
+                row_words = w_raw[k // PAIR][:, i, k % PAIR, :].bitcast(F32)
+                bank = psum_words.tile([P, SLICES, P], F32, tag="words")
+                words_ps[k, i] = bank
+                for t_slice in range(SLICES):
+                    nc.tensor.transpose(
+                        out=bank[:, t_slice, :],
+                        in_=row_words[:, t_slice * P : (t_slice + 1) * P],
+                        identity=ident[:],
+                    )
+
+        def copy_group_out(k):
+            grouped_k = grouped_pool.tile(
+                [P, HEADS_PER_LOAD, PASSES * P * PACK], BF16, tag="w_grouped", align_bytes=64
+            )
+            w_grouped[k] = grouped_k
+            for i in range(HEADS_PER_LOAD):
+                nc.scalar.copy(
+                    out=grouped_k[:, i, :].bitcast(F32).rearrange("q (g s u) -> q g s u", g=PASSES, u=2),
+                    in_=words_ps[k, i][:].rearrange("q (g u) s -> q g s u", g=PASSES),
+                )
+
+        def quantise_group(k):
+            codes_k = codes_pool.tile([P, HEADS_PER_LOAD, PASSES, P], U32, tag="w_codes", align_bytes=64)
+            scales_k = codes_pool.tile([P, HEADS_PER_LOAD, PASSES, P], U8, tag="w_scales", align_bytes=64)
+            w_codes[k] = codes_k
+            w_scales[k] = scales_k
+            nc.vector.quantize_mx(
+                out=codes_k[:].rearrange("q i g s -> q (i g s)").bitcast(FP8X4),
+                scales=scales_k[:].rearrange("q i g s -> q (i g s)"),
+                in_=w_grouped[k][:].rearrange("q i f -> q (i f)"),
+            )
+
+        def multiply_group(k):
+            first_head = HEADS_PER_LOAD * ((k // PAIR) % 2)
+            acc_k = psum_acc.tile([P, HEADS_PER_LOAD, P], F32, tag="acc")
+            acc[k] = acc_k
+            for i in range(HEADS_PER_LOAD):
+                h = first_head + i
+                for g in range(PASSES):
+                    nc.tensor.matmul_mx(
+                        out=acc_k[:, i, :],
+                        lhsT=w_codes[k][:, i, g, :].bitcast(FP8X4),
+                        lhsT_scale=w_scales[k][:, i, g, :],
+                        rhs=x_codes[:, g, h * P : (h + 1) * P].bitcast(FP8X4),
+                        rhs_scale=x_scales[:, g, h * P : (h + 1) * P],
+                        start=(g == 0),
+                        stop=(g == PASSES - 1),
+                    )
+
+        def finish_group(k):
+            a = k // (2 * PAIR)
+            e = k % PAIR
+            first_head = HEADS_PER_LOAD * ((k // PAIR) % 2)
+            if k % (2 * PAIR) == 0:
+                out_a = out_pool.tile([P, WINDOWS, PAIR, C], F32, tag="out_sb")
+                out_sb[a] = out_a
+            for i in range(HEADS_PER_LOAD):
+                h = first_head + i
+                nc.vector.scalar_tensor_tensor(
+                    out=out_sb[a][:, :, e, h * HEAD_DIM : (h + 1) * HEAD_DIM],
+                    in0=acc[k][:, i, :].rearrange("p (n d) -> p n d", n=WINDOWS),
+                    scalar=bias_col[:, h, a, e : e + 1],
+                    in1=x_sb[:, :, a, e * C + h * HEAD_DIM : e * C + (h + 1) * HEAD_DIM],
+                    op0=ALU.add,
+                    op1=ALU.add,
+                )
+            if k % (2 * PAIR) == 2 * PAIR - 1:
+                for n in range(WINDOWS):
+                    nc.sync.dma_start(
+                        out=out_windows[n // 2, n % 2, a], in_=out_sb[a][:, n].rearrange("p e c -> p (e c)")
+                    )
+
+        def prepare_group(k):
+            transpose_group(k)
+            copy_group_out(k)
+            if k % PAIR == PAIR - 1 and k // PAIR + WEIGHT_BUFS < LOADS:
+                load_weights(k // PAIR + WEIGHT_BUFS)
+
+        for n in range(WINDOWS):
+            for a in range(SLICES):
+                nc.sync.dma_start(out=x_sb[:, n, a, :], in_=x_windows[n // 2, n % 2, a])
+        for c in range(WEIGHT_BUFS):
+            load_weights(c)
+
+        make_identity(nc, ident[:])
+        nc.vector.memset(norm_rows[:], 0.0)
+        nc.vector.memset(ones[:], 1.0)
+        nc.scalar.dma_start(out=norm_rows[0:1, 0:C], in_=norm1_w.unsqueeze(0))
+        nc.scalar.dma_start(out=norm_rows[0:1, C : 2 * C], in_=norm1_b.unsqueeze(0))
+        norm_ps = psum_words.tile([P, 2 * C], F32, tag="words")
+        nc.tensor.matmul(out=norm_ps[:], lhsT=ones[:], rhs=norm_rows[:], start=True, stop=True)
+        nc.vector.memset(bias_rows[:], 0.0)
+        nc.scalar.dma_start(
+            out=bias_rows[0 : HEADS * SLICES, :], in_=spatial_b.rearrange("h (a w) -> (h a) w", a=SLICES)
+        )
+        bias_ps = psum_words.tile([P, SLICES, P], F32, tag="words")
+        nc.tensor.transpose(out=bias_ps[:, 0, :], in_=bias_rows[:].bitcast(F32), identity=ident[:])
+
+        statistics(0)
+        for n in range(1, WINDOWS):
+            statistics(n)
+            scales(n - 1)
+            normalise(n - 1)
+            if n == 1:
+                nc.scalar.copy(out=norm_bc[:], in_=norm_ps[:])
+        prepare_group(0)
+        gain_and_shift(0)
+        scales(WINDOWS - 1)
+        normalise(WINDOWS - 1)
+        for k in range(1, AHEAD):
+            prepare_group(k)
+        nc.scalar.copy(
+            out=bias_col[:].rearrange("p h a e -> p (h a e)"),
+            in_=bias_ps[:, 0, 0 : HEADS * SLICES].bitcast(BF16),
+        )
+        for n in range(1, WINDOWS):
+            gain_and_shift(n)
         for g in range(PASSES):
             nc.vector.quantize_mx(
                 out=x_codes[:, g, :].bitcast(FP8X4),
@@ -147,60 +275,11 @@ def tile_swinmlpblocknew_pa_kernel(tc, x, norm1_w, norm1_b, spatial_w, spatial_b
                 in_=xn_grouped[:, g].rearrange("q h n f -> q (h n f)"),
             )
 
-        for a in range(SLICES):
-            out_sb = out_pool.tile([P, WINDOWS, PAIR, C], F32)
-            for first_head in range(0, HEADS, HEADS_PER_LOAD):
-                w_raw = weight_pool.tile([P, HEADS_PER_LOAD, PAIR, TOKENS], BF16)
-                nc.sync.dma_start(
-                    out=w_raw[:].rearrange("p i e t -> p i (e t)"),
-                    in_=spatial_w[
-                        first_head : first_head + HEADS_PER_LOAD, PAIR * P * a : PAIR * P * (a + 1), :
-                    ].rearrange("i (p e) t -> p i (e t)", e=PAIR),
-                )
-                for e in range(PAIR):
-                    w_grouped = grouped_pool.tile([P, HEADS_PER_LOAD, PASSES * P * PACK], BF16, align_bytes=64)
-                    for i in range(HEADS_PER_LOAD):
-                        row_words = w_raw[:, i, e, :].bitcast(F32)
-                        words_ps = psum_words.tile([P, PACK, P], F32, tag="words")
-                        for k in range(SLICES):
-                            nc.tensor.transpose(
-                                out=words_ps[:, k, :], in_=row_words[:, k * P : (k + 1) * P], identity=ident[:]
-                            )
-                        nc.scalar.copy(
-                            out=w_grouped[:, i, :].bitcast(F32).rearrange("q (g s u) -> q g s u", g=PASSES, u=2),
-                            in_=words_ps[:].rearrange("q (g u) s -> q g s u", g=PASSES),
-                        )
-                    w_codes = codes_pool.tile([P, HEADS_PER_LOAD, PASSES, P], U32, align_bytes=64)
-                    w_scales = codes_pool.tile([P, HEADS_PER_LOAD, PASSES, P], U8, align_bytes=64)
-                    nc.vector.quantize_mx(
-                        out=w_codes[:].rearrange("q i g s -> q (i g s)").bitcast(FP8X4),
-                        scales=w_scales[:].rearrange("q i g s -> q (i g s)"),
-                        in_=w_grouped[:].rearrange("q i f -> q (i f)"),
-                    )
-                    acc = psum_acc.tile([P, HEADS_PER_LOAD, P], F32)
-                    for i in range(HEADS_PER_LOAD):
-                        h = first_head + i
-                        for g in range(PASSES):
-                            nc.tensor.matmul_mx(
-                                out=acc[:, i, :],
-                                lhsT=w_codes[:, i, g, :].bitcast(FP8X4),
-                                lhsT_scale=w_scales[:, i, g, :],
-                                rhs=x_codes[:, g, h * P : (h + 1) * P].bitcast(FP8X4),
-                                rhs_scale=x_scales[:, g, h * P : (h + 1) * P],
-                                start=(g == 0),
-                                stop=(g == PASSES - 1),
-                            )
-                    for i in range(HEADS_PER_LOAD):
-                        h = first_head + i
-                        nc.vector.scalar_tensor_tensor(
-                            out=out_sb[:, :, e, h * HEAD_DIM : (h + 1) * HEAD_DIM],
-                            in0=acc[:, i, :].rearrange("p (n d) -> p n d", n=WINDOWS),
-                            scalar=bias_col[:, h, a, e : e + 1],
-                            in1=x_sb[:, :, a, e * C + h * HEAD_DIM : e * C + (h + 1) * HEAD_DIM],
-                            op0=ALU.add,
-                            op1=ALU.add,
-                        )
-            for n in range(WINDOWS):
-                nc.sync.dma_start(
-                    out=out_windows[n // 2, n % 2, a], in_=out_sb[:, n].rearrange("p e c -> p (e c)")
-                )
+        for k in range(GROUPS):
+            quantise_group(k)
+            if k + AHEAD < GROUPS:
+                prepare_group(k + AHEAD)
+            multiply_group(k)
+            if k > 0:
+                finish_group(k - 1)
+        finish_group(GROUPS - 1)

@@ -25,26 +25,33 @@ HEADS_PER_LOAD = 4
 LOADS = SLICES * HEADS // HEADS_PER_LOAD
 GROUPS = LOADS * PAIR
 AHEAD = 4
-WEIGHT_BUFS = 5
+WEIGHT_BUFS = 4
 EPS = 1e-5
 
 FLOPS = 2 * HEADS * WINDOWS * TOKENS * TOKENS * HEAD_DIM
 
 
-def window_view(tokens_by_channels):
+def contraction_view(tokens_by_channels):
     return tokens_by_channels.rearrange(
         "b (wr a qh wc ql e) c -> (b wr) wc a qh ql (e c)", wr=2, a=SLICES, qh=8, wc=2, ql=16, e=PAIR
     )
 
 
+def output_view(tokens_by_channels):
+    return tokens_by_channels.rearrange(
+        "b (wr r wc pl a e) c -> (b wr) wc r pl a e c", wr=2, r=32, wc=2, pl=4, a=SLICES, e=PAIR
+    )
+
+
 def tile_swinmlpblocknew_pa_kernel(tc, x, norm1_w, norm1_b, spatial_w, spatial_b, out):
     nc = tc.nc
-    x_windows = window_view(x)
-    out_windows = window_view(out)
+    x_by_t = contraction_view(x)
+    x_by_s = output_view(x)
+    out_by_s = output_view(out)
 
     with ExitStack() as ctx:
         keep = ctx.enter_context(tc.tile_pool(name="keep", bufs=1))
-        norm_pool = ctx.enter_context(tc.tile_pool(name="norm", bufs=2))
+        norm_pool = ctx.enter_context(tc.tile_pool(name="norm", bufs=3))
         weight_pool = ctx.enter_context(tc.tile_pool(name="weights", bufs=WEIGHT_BUFS))
         grouped_pool = ctx.enter_context(tc.tile_pool(name="grouped", bufs=AHEAD))
         codes_pool = ctx.enter_context(tc.tile_pool(name="codes", bufs=3))
@@ -54,11 +61,12 @@ def tile_swinmlpblocknew_pa_kernel(tc, x, norm1_w, norm1_b, spatial_w, spatial_b
         ctx.enter_context(tc.manual_schedule())
 
         x_sb = keep.tile([P, WINDOWS, SLICES, PAIR * C], BF16)
+        x_res = keep.tile([P, WINDOWS, SLICES, PAIR * C], BF16)
         ident = keep.tile([P, P], F32)
         ones = keep.tile([P, P], BF16)
         norm_rows = keep.tile([P, 2 * C], BF16)
         norm_bc = keep.tile([P, 2 * C], F32)
-        bias_rows = keep.tile([P, PAIR * P], BF16)
+        bias_bf = keep.tile([P, HEADS, SLICES * PAIR], BF16)
         bias_col = keep.tile([P, HEADS, SLICES, PAIR], F32)
         stats = keep.tile([P, WINDOWS, SLICES, 3 * PAIR], F32)
         var_eps = keep.tile([P, WINDOWS, SLICES, PAIR], F32)
@@ -144,9 +152,9 @@ def tile_swinmlpblocknew_pa_kernel(tc, x, norm1_w, norm1_b, spatial_w, spatial_b
             w_raw[c] = w_raw_c
             nc.sync.dma_start(
                 out=w_raw_c[:].rearrange("p i e t -> p i (e t)"),
-                in_=spatial_w[
-                    first_head : first_head + HEADS_PER_LOAD, PAIR * P * a : PAIR * P * (a + 1), :
-                ].rearrange("i (p e) t -> p i (e t)", e=PAIR),
+                in_=spatial_w[first_head : first_head + HEADS_PER_LOAD].rearrange(
+                    "i (p a e) t -> a p i (e t)", a=SLICES, e=PAIR
+                )[a],
             )
 
         def transpose_group(k):
@@ -213,15 +221,13 @@ def tile_swinmlpblocknew_pa_kernel(tc, x, norm1_w, norm1_b, spatial_w, spatial_b
                     out=out_sb[a][:, :, e, h * HEAD_DIM : (h + 1) * HEAD_DIM],
                     in0=acc[k][:, i, :].rearrange("p (n d) -> p n d", n=WINDOWS),
                     scalar=bias_col[:, h, a, e : e + 1],
-                    in1=x_sb[:, :, a, e * C + h * HEAD_DIM : e * C + (h + 1) * HEAD_DIM],
+                    in1=x_res[:, :, a, e * C + h * HEAD_DIM : e * C + (h + 1) * HEAD_DIM],
                     op0=ALU.add,
                     op1=ALU.add,
                 )
-            if k % (2 * PAIR) == 2 * PAIR - 1:
+            if first_head + HEADS_PER_LOAD == HEADS:
                 for n in range(WINDOWS):
-                    nc.sync.dma_start(
-                        out=out_windows[n // 2, n % 2, a], in_=out_sb[a][:, n].rearrange("p e c -> p (e c)")
-                    )
+                    nc.sync.dma_start(out=out_by_s[n // 2, n % 2, :, :, a, e, :], in_=out_sb[a][:, n, e, :])
 
         def prepare_group(k):
             transpose_group(k)
@@ -231,9 +237,15 @@ def tile_swinmlpblocknew_pa_kernel(tc, x, norm1_w, norm1_b, spatial_w, spatial_b
 
         for n in range(WINDOWS):
             for a in range(SLICES):
-                nc.sync.dma_start(out=x_sb[:, n, a, :], in_=x_windows[n // 2, n % 2, a])
+                nc.sync.dma_start(out=x_sb[:, n, a, :], in_=x_by_t[n // 2, n % 2, a])
         for c in range(WEIGHT_BUFS):
             load_weights(c)
+            if c == 1:
+                for n in range(WINDOWS):
+                    nc.sync.dma_start(
+                        out=x_res[:, n].rearrange("p a f -> p (a f)"),
+                        in_=x_by_s[n // 2, n % 2].rearrange("r pl a e c -> r pl (a e c)"),
+                    )
 
         make_identity(nc, ident[:])
         nc.vector.memset(norm_rows[:], 0.0)
@@ -242,12 +254,7 @@ def tile_swinmlpblocknew_pa_kernel(tc, x, norm1_w, norm1_b, spatial_w, spatial_b
         nc.scalar.dma_start(out=norm_rows[0:1, C : 2 * C], in_=norm1_b.unsqueeze(0))
         norm_ps = psum_words.tile([P, 2 * C], F32, tag="words")
         nc.tensor.matmul(out=norm_ps[:], lhsT=ones[:], rhs=norm_rows[:], start=True, stop=True)
-        nc.vector.memset(bias_rows[:], 0.0)
-        nc.scalar.dma_start(
-            out=bias_rows[0 : HEADS * SLICES, :], in_=spatial_b.rearrange("h (a w) -> (h a) w", a=SLICES)
-        )
-        bias_ps = psum_words.tile([P, SLICES, P], F32, tag="words")
-        nc.tensor.transpose(out=bias_ps[:, 0, :], in_=bias_rows[:].bitcast(F32), identity=ident[:])
+        nc.scalar.dma_start(out=bias_bf[:], in_=spatial_b.rearrange("h (p i) -> p h i", i=SLICES * PAIR))
 
         statistics(0)
         for n in range(1, WINDOWS):
@@ -262,10 +269,7 @@ def tile_swinmlpblocknew_pa_kernel(tc, x, norm1_w, norm1_b, spatial_w, spatial_b
         normalise(WINDOWS - 1)
         for k in range(1, AHEAD):
             prepare_group(k)
-        nc.scalar.copy(
-            out=bias_col[:].rearrange("p h a e -> p (h a e)"),
-            in_=bias_ps[:, 0, 0 : HEADS * SLICES].bitcast(BF16),
-        )
+        nc.scalar.copy(out=bias_col[:].rearrange("p h a e -> p h (a e)"), in_=bias_bf[:])
         for n in range(1, WINDOWS):
             gain_and_shift(n)
         for g in range(PASSES):

@@ -65,7 +65,6 @@ def tile_swinmlpblocknew_pa_kernel(tc, x, norm1_w, norm1_b, spatial_w, spatial_b
         ident = keep.tile([P, P], F32)
         ones = keep.tile([P, P], BF16)
         norm_rows = keep.tile([P, 2 * C], BF16)
-        norm_bc = keep.tile([P, 2 * C], F32)
         bias_bf = keep.tile([P, HEADS, SLICES * PAIR], BF16)
         bias_col = keep.tile([P, HEADS, SLICES, PAIR], F32)
         stats = keep.tile([P, WINDOWS, SLICES, 3 * PAIR], F32)
@@ -131,14 +130,14 @@ def tile_swinmlpblocknew_pa_kernel(tc, x, norm1_w, norm1_b, spatial_w, spatial_b
             nc.vector.tensor_tensor(
                 out=normed[n][:],
                 in0=normed[n][:],
-                in1=norm_bc[:, 0:C].unsqueeze(1).to_broadcast([P, SLICES * PAIR, C]),
+                in1=norm_ps[:, 0:C].unsqueeze(1).to_broadcast([P, SLICES * PAIR, C]),
                 op=ALU.mult,
             )
             for g in range(PASSES):
                 nc.vector.tensor_tensor(
                     out=xn_grouped[:, g, :, n, :].rearrange("q h (d j) -> q h d j", j=PACK),
                     in0=normed[n][:, PACK * g : PACK * (g + 1), :].rearrange("q j (h d) -> q h d j", h=HEADS),
-                    in1=norm_bc[:, C : 2 * C]
+                    in1=norm_ps[:, C : 2 * C]
                     .rearrange("q (h d) -> q h d", h=HEADS)
                     .unsqueeze(3)
                     .to_broadcast([P, HEADS, HEAD_DIM, PACK]),
@@ -252,7 +251,7 @@ def tile_swinmlpblocknew_pa_kernel(tc, x, norm1_w, norm1_b, spatial_w, spatial_b
         nc.vector.memset(ones[:], 1.0)
         nc.scalar.dma_start(out=norm_rows[0:1, 0:C], in_=norm1_w.unsqueeze(0))
         nc.scalar.dma_start(out=norm_rows[0:1, C : 2 * C], in_=norm1_b.unsqueeze(0))
-        norm_ps = psum_words.tile([P, 2 * C], F32, tag="words")
+        norm_ps = psum_acc.tile([P, 2 * C], F32, tag="acc")
         nc.tensor.matmul(out=norm_ps[:], lhsT=ones[:], rhs=norm_rows[:], start=True, stop=True)
         nc.scalar.dma_start(out=bias_bf[:], in_=spatial_b.rearrange("h (p i) -> p h i", i=SLICES * PAIR))
 
@@ -261,8 +260,6 @@ def tile_swinmlpblocknew_pa_kernel(tc, x, norm1_w, norm1_b, spatial_w, spatial_b
             statistics(n)
             scales(n - 1)
             normalise(n - 1)
-            if n == 1:
-                nc.scalar.copy(out=norm_bc[:], in_=norm_ps[:])
         prepare_group(0)
         gain_and_shift(0)
         scales(WINDOWS - 1)

@@ -117,14 +117,21 @@ def tile_swinmlpblocknew_pa_kernel(tc, x, norm1_w, norm1_b, spatial_w, spatial_b
             normed_n = norm_pool.tile([P, SLICES * PAIR, C], F32, tag="normed")
             normed[n] = normed_n
             for a in range(SLICES):
-                for e in range(PAIR):
-                    nc.scalar.activation(
-                        out=normed_n[:, PAIR * a + e, :],
-                        in_=x_sb[:, n, a, e * C : (e + 1) * C],
-                        func=ACT.Identity,
-                        scale=rstd[:, n, a, e : e + 1],
-                        bias=minus_mean_rstd[:, n, a, e : e + 1],
-                    )
+                nc.scalar.activation(
+                    out=normed_n[:, PAIR * a, :],
+                    in_=x_sb[:, n, a, 0:C],
+                    func=ACT.Identity,
+                    scale=rstd[:, n, a, 0:1],
+                    bias=minus_mean_rstd[:, n, a, 0:1],
+                )
+                nc.gpsimd.tensor_scalar(
+                    out=normed_n[:, PAIR * a + 1, :],
+                    in0=x_sb[:, n, a, C : 2 * C],
+                    scalar1=rstd[:, n, a, 1:2],
+                    scalar2=minus_mean_rstd[:, n, a, 1:2],
+                    op0=ALU.mult,
+                    op1=ALU.add,
+                )
 
         def gain_and_shift(n):
             nc.vector.tensor_tensor(
@@ -260,11 +267,10 @@ def tile_swinmlpblocknew_pa_kernel(tc, x, norm1_w, norm1_b, spatial_w, spatial_b
             statistics(n)
             scales(n - 1)
             normalise(n - 1)
-        prepare_group(0)
         gain_and_shift(0)
         scales(WINDOWS - 1)
         normalise(WINDOWS - 1)
-        for k in range(1, AHEAD):
+        for k in range(AHEAD):
             prepare_group(k)
         nc.scalar.copy(out=bias_col[:].rearrange("p h a e -> p h (a e)"), in_=bias_bf[:])
         for n in range(1, WINDOWS):

from contextlib import ExitStack

import concourse.mybir as mybir
from concourse.masks import make_identity

F32 = mybir.dt.float32
BF16 = mybir.dt.bfloat16
U32 = mybir.dt.uint32
U8 = mybir.dt.uint8
FP8X4 = mybir.dt.float8_e4m3fn_x4
ALU = mybir.AluOpType
ACT = mybir.ActivationFunctionType

P = 128
C = 256
HEADS = 8
HEAD_DIM = C // HEADS
WINDOWS = 4
TOKENS = 1024
PAIR = 2
SLICES = TOKENS // (PAIR * P)
PASSES = 2
PACK = 4
HEADS_PER_LOAD = 4
LOADS = SLICES * HEADS // HEADS_PER_LOAD
GROUPS = LOADS * PAIR
AHEAD = 4
WEIGHT_BUFS = 4
EPS = 1e-5

FLOPS = 2 * HEADS * WINDOWS * TOKENS * TOKENS * HEAD_DIM


def contraction_view(tokens_by_channels):
    return tokens_by_channels.rearrange(
        "b (wr a qh wc ql e) c -> (b wr) wc a qh ql (e c)", wr=2, a=SLICES, qh=8, wc=2, ql=16, e=PAIR
    )


def output_view(tokens_by_channels):
    return tokens_by_channels.rearrange(
        "b (wr r wc pl a e) c -> (b wr) wc r pl a e c", wr=2, r=32, wc=2, pl=4, a=SLICES, e=PAIR
    )


def tile_swinmlpblocknew_pa_kernel(tc, x, norm1_w, norm1_b, spatial_w, spatial_b, out):
    nc = tc.nc
    x_by_t = contraction_view(x)
    x_by_s = output_view(x)
    out_by_s = output_view(out)

    with ExitStack() as ctx:
        keep = ctx.enter_context(tc.tile_pool(name="keep", bufs=1))
        norm_pool = ctx.enter_context(tc.tile_pool(name="norm", bufs=3))
        weight_pool = ctx.enter_context(tc.tile_pool(name="weights", bufs=WEIGHT_BUFS))
        grouped_pool = ctx.enter_context(tc.tile_pool(name="grouped", bufs=AHEAD))
        codes_pool = ctx.enter_context(tc.tile_pool(name="codes", bufs=3))
        out_pool = ctx.enter_context(tc.tile_pool(name="outs", bufs=2))
        psum_words = ctx.enter_context(tc.psum_pool(name="psum_words", bufs=6))
        psum_acc = ctx.enter_context(tc.psum_pool(name="psum_acc", bufs=2))
        ctx.enter_context(tc.manual_schedule())

        x_sb = keep.tile([P, WINDOWS, SLICES, PAIR * C], BF16)
        x_res = keep.tile([P, WINDOWS, SLICES, PAIR * C], BF16)
        ident = keep.tile([P, P], F32)
        ones = keep.tile([P, P], BF16)
        norm_rows = keep.tile([P, 2 * C], BF16)
        bias_bf = keep.tile([P, HEADS, SLICES * PAIR], BF16)
        bias_col = keep.tile([P, HEADS, SLICES, PAIR], F32)
        stats = keep.tile([P, WINDOWS, SLICES, 3 * PAIR], F32)
        var_eps = keep.tile([P, WINDOWS, SLICES, PAIR], F32)
        std = keep.tile([P, WINDOWS, SLICES, PAIR], F32)
        rstd = keep.tile([P, WINDOWS, SLICES, PAIR], F32)
        minus_mean_rstd = keep.tile([P, WINDOWS, SLICES, PAIR], F32)
        xn_grouped = keep.tile([P, PASSES, HEADS, WINDOWS, HEAD_DIM * PACK], BF16, align_bytes=64)
        x_codes = keep.tile([P, PASSES, HEADS * P], U32, align_bytes=64)
        x_scales = keep.tile([P, PASSES, HEADS * P], U8, align_bytes=64)

        normed = {}
        w_raw = {}
        words_ps = {}
        w_grouped = {}
        w_codes = {}
        w_scales = {}
        acc = {}
        out_sb = {}

        def statistics(n):
            for a in range(SLICES):
                nc.vector.bn_stats(
                    out=stats[:, n, a, :], in_=x_sb[:, n, a, :].rearrange("q (e c) -> q c e", e=PAIR)
                )
            moments = stats[:, n, :, :].rearrange("q a (e k) -> q a e k", k=3)
            nc.vector.tensor_scalar(
                out=var_eps[:, n],
                in0=moments[:, :, :, 2],
                scalar1=1.0 / C,
                scalar2=EPS,
                op0=ALU.mult,
                op1=ALU.add,
            )
            nc.scalar.sqrt(out=std[:, n], in_=var_eps[:, n])

        def scales(n):
            moments = stats[:, n, :, :].rearrange("q a (e k) -> q a e k", k=3)
            nc.vector.reciprocal(out=rstd[:, n], in_=std[:, n])
            nc.vector.scalar_tensor_tensor(
                out=minus_mean_rstd[:, n],
                in0=moments[:, :, :, 1],
                scalar=-1.0,
                in1=rstd[:, n],
                op0=ALU.mult,
                op1=ALU.mult,
            )

        def normalise(n):
            normed_n = norm_pool.tile([P, SLICES * PAIR, C], F32, tag="normed")
            normed[n] = normed_n
            for a in range(SLICES):
                nc.scalar.activation(
                    out=normed_n[:, PAIR * a, :],
                    in_=x_sb[:, n, a, 0:C],
                    func=ACT.Identity,
                    scale=rstd[:, n, a, 0:1],
                    bias=minus_mean_rstd[:, n, a, 0:1],
                )
                nc.gpsimd.tensor_scalar(
                    out=normed_n[:, PAIR * a + 1, :],
                    in0=x_sb[:, n, a, C : 2 * C],
                    scalar1=rstd[:, n, a, 1:2],
                    scalar2=minus_mean_rstd[:, n, a, 1:2],
                    op0=ALU.mult,
                    op1=ALU.add,
                )

        def gain_and_shift(n):
            nc.vector.tensor_tensor(
                out=normed[n][:],
                in0=normed[n][:],
                in1=norm_ps[:, 0:C].unsqueeze(1).to_broadcast([P, SLICES * PAIR, C]),
                op=ALU.mult,
            )
            for g in range(PASSES):
                nc.vector.tensor_tensor(
                    out=xn_grouped[:, g, :, n, :].rearrange("q h (d j) -> q h d j", j=PACK),
                    in0=normed[n][:, PACK * g : PACK * (g + 1), :].rearrange("q j (h d) -> q h d j", h=HEADS),
                    in1=norm_ps[:, C : 2 * C]
                    .rearrange("q (h d) -> q h d", h=HEADS)
                    .unsqueeze(3)
                    .to_broadcast([P, HEADS, HEAD_DIM, PACK]),
                    op=ALU.add,
                )

        def load_weights(c):
            a = c // 2
            first_head = HEADS_PER_LOAD * (c % 2)
            w_raw_c = weight_pool.tile([P, HEADS_PER_LOAD, PAIR, TOKENS], BF16, tag="w_raw")
            w_raw[c] = w_raw_c
            nc.sync.dma_start(
                out=w_raw_c[:].rearrange("p i e t -> p i (e t)"),
                in_=spatial_w[first_head : first_head + HEADS_PER_LOAD].rearrange(
                    "i (p a e) t -> a p i (e t)", a=SLICES, e=PAIR
                )[a],
            )

        def transpose_group(k):
            for i in range(HEADS_PER_LOAD):
                row_words = w_raw[k // PAIR][:, i, k % PAIR, :].bitcast(F32)
                bank = psum_words.tile([P, SLICES, P], F32, tag="words")
                words_ps[k, i] = bank
                for t_slice in range(SLICES):
                    nc.tensor.transpose(
                        out=bank[:, t_slice, :],
                        in_=row_words[:, t_slice * P : (t_slice + 1) * P],
                        identity=ident[:],
                    )

        def copy_group_out(k):
            grouped_k = grouped_pool.tile(
                [P, HEADS_PER_LOAD, PASSES * P * PACK], BF16, tag="w_grouped", align_bytes=64
            )
            w_grouped[k] = grouped_k
            for i in range(HEADS_PER_LOAD):
                nc.scalar.copy(
                    out=grouped_k[:, i, :].bitcast(F32).rearrange("q (g s u) -> q g s u", g=PASSES, u=2),
                    in_=words_ps[k, i][:].rearrange("q (g u) s -> q g s u", g=PASSES),
                )

        def quantise_group(k):
            codes_k = codes_pool.tile([P, HEADS_PER_LOAD, PASSES, P], U32, tag="w_codes", align_bytes=64)
            scales_k = codes_pool.tile([P, HEADS_PER_LOAD, PASSES, P], U8, tag="w_scales", align_bytes=64)
            w_codes[k] = codes_k
            w_scales[k] = scales_k
            nc.vector.quantize_mx(
                out=codes_k[:].rearrange("q i g s -> q (i g s)").bitcast(FP8X4),
                scales=scales_k[:].rearrange("q i g s -> q (i g s)"),
                in_=w_grouped[k][:].rearrange("q i f -> q (i f)"),
            )

        def multiply_group(k):
            first_head = HEADS_PER_LOAD * ((k // PAIR) % 2)
            acc_k = psum_acc.tile([P, HEADS_PER_LOAD, P], F32, tag="acc")
            acc[k] = acc_k
            for i in range(HEADS_PER_LOAD):
                h = first_head + i
                for g in range(PASSES):
                    nc.tensor.matmul_mx(
                        out=acc_k[:, i, :],
                        lhsT=w_codes[k][:, i, g, :].bitcast(FP8X4),
                        lhsT_scale=w_scales[k][:, i, g, :],
                        rhs=x_codes[:, g, h * P : (h + 1) * P].bitcast(FP8X4),
                        rhs_scale=x_scales[:, g, h * P : (h + 1) * P],
                        start=(g == 0),
                        stop=(g == PASSES - 1),
                    )

        def finish_group(k):
            a = k // (2 * PAIR)
            e = k % PAIR
            first_head = HEADS_PER_LOAD * ((k // PAIR) % 2)
            if k % (2 * PAIR) == 0:
                out_a = out_pool.tile([P, WINDOWS, PAIR, C], F32, tag="out_sb")
                out_sb[a] = out_a
            for i in range(HEADS_PER_LOAD):
                h = first_head + i
                nc.vector.scalar_tensor_tensor(
                    out=out_sb[a][:, :, e, h * HEAD_DIM : (h + 1) * HEAD_DIM],
                    in0=acc[k][:, i, :].rearrange("p (n d) -> p n d", n=WINDOWS),
                    scalar=bias_col[:, h, a, e : e + 1],
                    in1=x_res[:, :, a, e * C + h * HEAD_DIM : e * C + (h + 1) * HEAD_DIM],
                    op0=ALU.add,
                    op1=ALU.add,
                )
            if first_head + HEADS_PER_LOAD == HEADS:
                for n in range(WINDOWS):
                    nc.sync.dma_start(out=out_by_s[n // 2, n % 2, :, :, a, e, :], in_=out_sb[a][:, n, e, :])

        def prepare_group(k):
            transpose_group(k)
            copy_group_out(k)
            if k % PAIR == PAIR - 1 and k // PAIR + WEIGHT_BUFS < LOADS:
                load_weights(k // PAIR + WEIGHT_BUFS)

        for n in range(WINDOWS):
            for a in range(SLICES):
                nc.sync.dma_start(out=x_sb[:, n, a, :], in_=x_by_t[n // 2, n % 2, a])
        for c in range(WEIGHT_BUFS):
            load_weights(c)
            if c == 1:
                for n in range(WINDOWS):
                    nc.sync.dma_start(
                        out=x_res[:, n].rearrange("p a f -> p (a f)"),
                        in_=x_by_s[n // 2, n % 2].rearrange("r pl a e c -> r pl (a e c)"),
                    )

        make_identity(nc, ident[:])
        nc.vector.memset(norm_rows[:], 0.0)
        nc.vector.memset(ones[:], 1.0)
        nc.scalar.dma_start(out=norm_rows[0:1, 0:C], in_=norm1_w.unsqueeze(0))
        nc.scalar.dma_start(out=norm_rows[0:1, C : 2 * C], in_=norm1_b.unsqueeze(0))
        norm_ps = psum_acc.tile([P, 2 * C], F32, tag="acc")
        nc.tensor.matmul(out=norm_ps[:], lhsT=ones[:], rhs=norm_rows[:], start=True, stop=True)
        nc.scalar.dma_start(out=bias_bf[:], in_=spatial_b.rearrange("h (p i) -> p h i", i=SLICES * PAIR))

        statistics(0)
        for n in range(1, WINDOWS):
            statistics(n)
            scales(n - 1)
            normalise(n - 1)
        gain_and_shift(0)
        scales(WINDOWS - 1)
        normalise(WINDOWS - 1)
        for k in range(AHEAD):
            prepare_group(k)
        nc.scalar.copy(out=bias_col[:].rearrange("p h a e -> p h (a e)"), in_=bias_bf[:])
        for n in range(1, WINDOWS):
            gain_and_shift(n)
        for g in range(PASSES):
            nc.vector.quantize_mx(
                out=x_codes[:, g, :].bitcast(FP8X4),
                scales=x_scales[:, g, :],
                in_=xn_grouped[:, g].rearrange("q h n f -> q (h n f)"),
            )

        for k in range(GROUPS):
            quantise_group(k)
            if k + AHEAD < GROUPS:
                prepare_group(k + AHEAD)
            multiply_group(k)
            if k > 0:
                finish_group(k - 1)
        finish_group(GROUPS - 1)
